import numpy as np
import ml_dtypes

BF16 = ml_dtypes.bfloat16


def bf(x):
    return np.asarray(x, np.float32).astype(BF16)


def f32(x):
    return np.asarray(x, np.float32)


def f64(x):
    return np.asarray(x).astype(np.float64)


def striped(idx):
    return np.tile(idx.reshape(-1, 16).T, (8, 1))


C, S, N, F = 1024, 1024, 256, 512
THR = 0.03
TAU = 20.0
FREQ = 4.0
TT = 62
DEC = np.exp(-1.0 / TAU)
BIAS = 0.5 * np.sin(2.0 * np.pi * FREQ * (0.001 * TT))


def setup_inputs():
    return {
        "base": f32(0.2 * np.random.standard_normal((C, S))),
        "x": bf(4.0 * np.random.standard_normal((F, C))),
        "w": bf(np.random.standard_normal((F, N)) / np.sqrt(F)),
        "old_v": f32(0.2 * np.random.standard_normal((C, N))),
        "old_spike": f32(np.random.random((C, N)) < 0.5),
        "offs": striped(np.random.permutation(S)[:N]),
    }


def reference(base, x, w, old_v, old_spike, offs):
    idx = offs[:16].T.reshape(-1)
    a = DEC * f64(old_v) + (-THR) * f64(old_spike)
    b = (1.0 - DEC) * (f64(x).T @ f64(w) + BIAS)
    out = f64(base).copy()
    out[:, idx] = a + b
    return out

@@ -1,0 +1,68 @@
+import concourse.mybir as mybir
+
+P = 128
+C, S, N, F = 1024, 1024, 256, 512
+SAMPLE_BLOCKS = C // P
+FEATURE_BLOCKS = F // P
+
+DECAY = 0.951229424500714
+LEAK = 1.0 - DECAY
+RESET = -0.03
+BIAS = 0.49996052210190806
+
+FLOPS = 2 * C * N * F
+
+BF16, F32, U16 = mybir.dt.bfloat16, mybir.dt.float32, mybir.dt.uint16
+MULT, ADD = mybir.AluOpType.mult, mybir.AluOpType.add
+COPY = mybir.ActivationFunctionType.Copy
+
+
+def tile_rsnn_kernel(tc, base, x, w, old_v, old_spike, offs, out):
+    nc = tc.nc
+    base_blocks = base.rearrange("(i p) s -> i p s", p=P)
+    out_blocks = out.rearrange("(i p) s -> i p s", p=P)
+
+    with (
+        tc.tile_pool(name="held", bufs=1) as held,
+        tc.tile_pool(name="windows", bufs=SAMPLE_BLOCKS) as windows,
+        tc.tile_pool(name="work", bufs=3) as work,
+        tc.psum_pool(name="psum", bufs=4) as psum,
+    ):
+        offsets = held.tile([P, N // 16], U16, name="offsets")
+        nc.sync.dma_start(offsets[:], offs)
+
+        w_sb = held.tile([P, FEATURE_BLOCKS, N], BF16, name="w_sb")
+        nc.sync.dma_start(w_sb[:], w.rearrange("(p k) n -> p k n", k=FEATURE_BLOCKS))
+        x_sb = held.tile([P, FEATURE_BLOCKS, C], BF16, name="x_sb")
+        nc.scalar.dma_start(x_sb[:], x.rearrange("(p k) c -> p k c", k=FEATURE_BLOCKS))
+
+        v_sb = held.tile([P, SAMPLE_BLOCKS, N], F32, name="v_sb")
+        nc.sync.dma_start(v_sb[:], old_v.rearrange("(i p) n -> p i n", p=P))
+        spike_sb = held.tile([P, SAMPLE_BLOCKS, N], F32, name="spike_sb")
+        nc.scalar.dma_start(spike_sb[:], old_spike.rearrange("(i p) n -> p i n", p=P))
+
+        window_of = []
+        for i in range(SAMPLE_BLOCKS):
+            window = windows.tile([P, S], F32, name="window")
+            load_queue = nc.sync if i % 2 == 0 else nc.scalar
+            load_queue.dma_start(window[:], base_blocks[i])
+            window_of.append(window)
+
+        for i in range(SAMPLE_BLOCKS):
+            current = psum.tile([P, N], F32, name="current")
+            for k in range(FEATURE_BLOCKS):
+                nc.tensor.matmul(
+                    current[:],
+                    x_sb[:, k, i * P : (i + 1) * P],
+                    w_sb[:, k, :],
+                    start=(k == 0),
+                    stop=(k == FEATURE_BLOCKS - 1),
+                )
+            b = work.tile([P, N], F32, name="b")
+            nc.scalar.activation(b[:], current[:], COPY, bias=LEAK * BIAS, scale=LEAK)
+            reset = work.tile([P, N], F32, name="reset")
+            nc.scalar.mul(reset[:], spike_sb[:, i, :], RESET)
+            a = work.tile([P, N], F32, name="a")
+            nc.vector.scalar_tensor_tensor(a[:], v_sb[:, i, :], DECAY, reset[:], MULT, ADD)
+            nc.vector.tensor_tensor(window_of[i][:].indirect(offsets[:]), a[:], b[:], ADD)
+            nc.sync.dma_start(out_blocks[i], window_of[i][:])

@@ -21,10 +21,12 @@ def tile_rsnn_kernel(tc, base, x, w, old_v, old_spike, offs, out):
     nc = tc.nc
     base_blocks = base.rearrange("(i p) s -> i p s", p=P)
     out_blocks = out.rearrange("(i p) s -> i p s", p=P)
+    v_blocks = old_v.rearrange("(i p) n -> i p n", p=P)
+    spike_blocks = old_spike.rearrange("(i p) n -> i p n", p=P)
 
     with (
         tc.tile_pool(name="held", bufs=1) as held,
-        tc.tile_pool(name="windows", bufs=SAMPLE_BLOCKS) as windows,
+        tc.tile_pool(name="inputs", bufs=SAMPLE_BLOCKS) as inputs,
         tc.tile_pool(name="work", bufs=3) as work,
         tc.psum_pool(name="psum", bufs=4) as psum,
     ):
@@ -36,16 +38,16 @@ def tile_rsnn_kernel(tc, base, x, w, old_v, old_spike, offs, out):
         x_sb = held.tile([P, FEATURE_BLOCKS, C], BF16, name="x_sb")
         nc.scalar.dma_start(x_sb[:], x.rearrange("(p k) c -> p k c", k=FEATURE_BLOCKS))
 
-        v_sb = held.tile([P, SAMPLE_BLOCKS, N], F32, name="v_sb")
-        nc.sync.dma_start(v_sb[:], old_v.rearrange("(i p) n -> p i n", p=P))
-        spike_sb = held.tile([P, SAMPLE_BLOCKS, N], F32, name="spike_sb")
-        nc.scalar.dma_start(spike_sb[:], old_spike.rearrange("(i p) n -> p i n", p=P))
-
-        window_of = []
+        v_of, spike_of, window_of = [], [], []
         for i in range(SAMPLE_BLOCKS):
-            window = windows.tile([P, S], F32, name="window")
-            load_queue = nc.sync if i % 2 == 0 else nc.scalar
-            load_queue.dma_start(window[:], base_blocks[i])
+            spike = inputs.tile([P, N], F32, name="spike")
+            nc.scalar.dma_start(spike[:], spike_blocks[i])
+            v = inputs.tile([P, N], F32, name="v")
+            nc.sync.dma_start(v[:], v_blocks[i])
+            window = inputs.tile([P, S], F32, name="window")
+            nc.sync.dma_start(window[:], base_blocks[i])
+            spike_of.append(spike)
+            v_of.append(v)
             window_of.append(window)
 
         for i in range(SAMPLE_BLOCKS):
@@ -61,8 +63,8 @@ def tile_rsnn_kernel(tc, base, x, w, old_v, old_spike, offs, out):
             b = work.tile([P, N], F32, name="b")
             nc.scalar.activation(b[:], current[:], COPY, bias=LEAK * BIAS, scale=LEAK)
             reset = work.tile([P, N], F32, name="reset")
-            nc.scalar.mul(reset[:], spike_sb[:, i, :], RESET)
+            nc.scalar.mul(reset[:], spike_of[i][:], RESET)
             a = work.tile([P, N], F32, name="a")
-            nc.vector.scalar_tensor_tensor(a[:], v_sb[:, i, :], DECAY, reset[:], MULT, ADD)
+            nc.vector.scalar_tensor_tensor(a[:], v_of[i][:], DECAY, reset[:], MULT, ADD)
             nc.vector.tensor_tensor(window_of[i][:].indirect(offsets[:]), a[:], b[:], ADD)
             nc.sync.dma_start(out_blocks[i], window_of[i][:])

@@ -36,12 +36,12 @@ def tile_rsnn_kernel(tc, base, x, w, old_v, old_spike, offs, out):
         w_sb = held.tile([P, FEATURE_BLOCKS, N], BF16, name="w_sb")
         nc.sync.dma_start(w_sb[:], w.rearrange("(p k) n -> p k n", k=FEATURE_BLOCKS))
         x_sb = held.tile([P, FEATURE_BLOCKS, C], BF16, name="x_sb")
-        nc.scalar.dma_start(x_sb[:], x.rearrange("(p k) c -> p k c", k=FEATURE_BLOCKS))
+        nc.sync.dma_start(x_sb[:], x.rearrange("(p k) c -> p k c", k=FEATURE_BLOCKS))
 
         v_of, spike_of, window_of = [], [], []
         for i in range(SAMPLE_BLOCKS):
             spike = inputs.tile([P, N], F32, name="spike")
-            nc.scalar.dma_start(spike[:], spike_blocks[i])
+            nc.sync.dma_start(spike[:], spike_blocks[i])
             v = inputs.tile([P, N], F32, name="v")
             nc.sync.dma_start(v[:], v_blocks[i])
             window = inputs.tile([P, S], F32, name="window")

@@ -4,6 +4,7 @@ P = 128
 C, S, N, F = 1024, 1024, 256, 512
 SAMPLE_BLOCKS = C // P
 FEATURE_BLOCKS = F // P
+HALF = SAMPLE_BLOCKS // 2
 
 DECAY = 0.951229424500714
 LEAK = 1.0 - DECAY
@@ -19,14 +20,15 @@ COPY = mybir.ActivationFunctionType.Copy
 
 def tile_rsnn_kernel(tc, base, x, w, old_v, old_spike, offs, out):
     nc = tc.nc
-    base_blocks = base.rearrange("(i p) s -> i p s", p=P)
-    out_blocks = out.rearrange("(i p) s -> i p s", p=P)
-    v_blocks = old_v.rearrange("(i p) n -> i p n", p=P)
-    spike_blocks = old_spike.rearrange("(i p) n -> i p n", p=P)
+    base_blocks = base.rearrange("(p i) s -> i p s", i=SAMPLE_BLOCKS)
+    out_blocks = out.rearrange("(p i) s -> i p s", i=SAMPLE_BLOCKS)
+    v_rows = old_v.rearrange("(p i) n -> p i n", i=SAMPLE_BLOCKS)
+    spike_rows = old_spike.rearrange("(p i) n -> p i n", i=SAMPLE_BLOCKS)
 
     with (
         tc.tile_pool(name="held", bufs=1) as held,
-        tc.tile_pool(name="inputs", bufs=SAMPLE_BLOCKS) as inputs,
+        tc.tile_pool(name="halves", bufs=2) as halves,
+        tc.tile_pool(name="windows", bufs=SAMPLE_BLOCKS) as windows,
         tc.tile_pool(name="work", bufs=3) as work,
         tc.psum_pool(name="psum", bufs=4) as psum,
     ):
@@ -36,26 +38,28 @@ def tile_rsnn_kernel(tc, base, x, w, old_v, old_spike, offs, out):
         w_sb = held.tile([P, FEATURE_BLOCKS, N], BF16, name="w_sb")
         nc.sync.dma_start(w_sb[:], w.rearrange("(p k) n -> p k n", k=FEATURE_BLOCKS))
         x_sb = held.tile([P, FEATURE_BLOCKS, C], BF16, name="x_sb")
-        nc.sync.dma_start(x_sb[:], x.rearrange("(p k) c -> p k c", k=FEATURE_BLOCKS))
+        nc.scalar.dma_start(x_sb[:], x.rearrange("(p k) c -> p k c", k=FEATURE_BLOCKS))
+        x_by_block = x_sb[:].rearrange("p k (c i) -> p k i c", i=SAMPLE_BLOCKS)
 
         v_of, spike_of, window_of = [], [], []
-        for i in range(SAMPLE_BLOCKS):
-            spike = inputs.tile([P, N], F32, name="spike")
-            nc.sync.dma_start(spike[:], spike_blocks[i])
-            v = inputs.tile([P, N], F32, name="v")
-            nc.sync.dma_start(v[:], v_blocks[i])
-            window = inputs.tile([P, S], F32, name="window")
-            nc.sync.dma_start(window[:], base_blocks[i])
-            spike_of.append(spike)
-            v_of.append(v)
-            window_of.append(window)
+        for h in range(SAMPLE_BLOCKS // HALF):
+            v_half = halves.tile([P, HALF, N], F32, name="v_half")
+            nc.sync.dma_start(v_half[:], v_rows[:, h * HALF : (h + 1) * HALF, :])
+            spike_half = halves.tile([P, HALF, N], F32, name="spike_half")
+            nc.scalar.dma_start(spike_half[:], spike_rows[:, h * HALF : (h + 1) * HALF, :])
+            for j in range(HALF):
+                window = windows.tile([P, S], F32, name="window")
+                nc.sync.dma_start(window[:], base_blocks[h * HALF + j])
+                v_of.append(v_half[:, j, :])
+                spike_of.append(spike_half[:, j, :])
+                window_of.append(window)
 
         for i in range(SAMPLE_BLOCKS):
             current = psum.tile([P, N], F32, name="current")
             for k in range(FEATURE_BLOCKS):
                 nc.tensor.matmul(
                     current[:],
-                    x_sb[:, k, i * P : (i + 1) * P],
+                    x_by_block[:, k, i, :],
                     w_sb[:, k, :],
                     start=(k == 0),
                     stop=(k == FEATURE_BLOCKS - 1),
@@ -63,8 +67,8 @@ def tile_rsnn_kernel(tc, base, x, w, old_v, old_spike, offs, out):
             b = work.tile([P, N], F32, name="b")
             nc.scalar.activation(b[:], current[:], COPY, bias=LEAK * BIAS, scale=LEAK)
             reset = work.tile([P, N], F32, name="reset")
-            nc.scalar.mul(reset[:], spike_of[i][:], RESET)
+            nc.scalar.mul(reset[:], spike_of[i], RESET)
             a = work.tile([P, N], F32, name="a")
-            nc.vector.scalar_tensor_tensor(a[:], v_of[i][:], DECAY, reset[:], MULT, ADD)
+            nc.vector.scalar_tensor_tensor(a[:], v_of[i], DECAY, reset[:], MULT, ADD)
             nc.vector.tensor_tensor(window_of[i][:].indirect(offsets[:]), a[:], b[:], ADD)
             nc.sync.dma_start(out_blocks[i], window_of[i][:])

@@ -29,6 +29,7 @@ def tile_rsnn_kernel(tc, base, x, w, old_v, old_spike, offs, out):
         tc.tile_pool(name="held", bufs=1) as held,
         tc.tile_pool(name="halves", bufs=2) as halves,
         tc.tile_pool(name="windows", bufs=SAMPLE_BLOCKS) as windows,
+        tc.tile_pool(name="terms", bufs=SAMPLE_BLOCKS) as terms,
         tc.tile_pool(name="work", bufs=3) as work,
         tc.psum_pool(name="psum", bufs=4) as psum,
     ):
@@ -54,6 +55,7 @@ def tile_rsnn_kernel(tc, base, x, w, old_v, old_spike, offs, out):
                 spike_of.append(spike_half[:, j, :])
                 window_of.append(window)
 
+        b_of, reset_of = [], []
         for i in range(SAMPLE_BLOCKS):
             current = psum.tile([P, N], F32, name="current")
             for k in range(FEATURE_BLOCKS):
@@ -64,11 +66,16 @@ def tile_rsnn_kernel(tc, base, x, w, old_v, old_spike, offs, out):
                     start=(k == 0),
                     stop=(k == FEATURE_BLOCKS - 1),
                 )
-            b = work.tile([P, N], F32, name="b")
+            b = terms.tile([P, N], F32, name="b")
             nc.scalar.activation(b[:], current[:], COPY, bias=LEAK * BIAS, scale=LEAK)
-            reset = work.tile([P, N], F32, name="reset")
+            reset = terms.tile([P, N], F32, name="reset")
             nc.scalar.mul(reset[:], spike_of[i], RESET)
+            b_of.append(b)
+            reset_of.append(reset)
+
+        for i in range(SAMPLE_BLOCKS):
             a = work.tile([P, N], F32, name="a")
-            nc.vector.scalar_tensor_tensor(a[:], v_of[i], DECAY, reset[:], MULT, ADD)
-            nc.vector.tensor_tensor(window_of[i][:].indirect(offsets[:]), a[:], b[:], ADD)
-            nc.sync.dma_start(out_blocks[i], window_of[i][:])
+            nc.vector.scalar_tensor_tensor(a[:], v_of[i], DECAY, reset_of[i][:], MULT, ADD)
+            nc.vector.tensor_tensor(window_of[i][:].indirect(offsets[:]), a[:], b_of[i][:], ADD)
+            store_queue = nc.sync if i % 2 == 0 else nc.scalar
+            store_queue.dma_start(out_blocks[i], window_of[i][:])

@@ -4,7 +4,7 @@ P = 128
 C, S, N, F = 1024, 1024, 256, 512
 SAMPLE_BLOCKS = C // P
 FEATURE_BLOCKS = F // P
-HALF = SAMPLE_BLOCKS // 2
+GROUP = 2
 
 DECAY = 0.951229424500714
 LEAK = 1.0 - DECAY
@@ -27,9 +27,8 @@ def tile_rsnn_kernel(tc, base, x, w, old_v, old_spike, offs, out):
 
     with (
         tc.tile_pool(name="held", bufs=1) as held,
-        tc.tile_pool(name="halves", bufs=2) as halves,
+        tc.tile_pool(name="groups", bufs=SAMPLE_BLOCKS // GROUP) as groups,
         tc.tile_pool(name="windows", bufs=SAMPLE_BLOCKS) as windows,
-        tc.tile_pool(name="terms", bufs=SAMPLE_BLOCKS) as terms,
         tc.tile_pool(name="work", bufs=3) as work,
         tc.psum_pool(name="psum", bufs=4) as psum,
     ):
@@ -43,19 +42,18 @@ def tile_rsnn_kernel(tc, base, x, w, old_v, old_spike, offs, out):
         x_by_block = x_sb[:].rearrange("p k (c i) -> p k i c", i=SAMPLE_BLOCKS)
 
         v_of, spike_of, window_of = [], [], []
-        for h in range(SAMPLE_BLOCKS // HALF):
-            v_half = halves.tile([P, HALF, N], F32, name="v_half")
-            nc.sync.dma_start(v_half[:], v_rows[:, h * HALF : (h + 1) * HALF, :])
-            spike_half = halves.tile([P, HALF, N], F32, name="spike_half")
-            nc.scalar.dma_start(spike_half[:], spike_rows[:, h * HALF : (h + 1) * HALF, :])
-            for j in range(HALF):
+        for g in range(SAMPLE_BLOCKS // GROUP):
+            v_group = groups.tile([P, GROUP, N], F32, name="v_group")
+            nc.sync.dma_start(v_group[:], v_rows[:, g * GROUP : (g + 1) * GROUP, :])
+            spike_group = groups.tile([P, GROUP, N], F32, name="spike_group")
+            nc.scalar.dma_start(spike_group[:], spike_rows[:, g * GROUP : (g + 1) * GROUP, :])
+            for j in range(GROUP):
                 window = windows.tile([P, S], F32, name="window")
-                nc.sync.dma_start(window[:], base_blocks[h * HALF + j])
-                v_of.append(v_half[:, j, :])
-                spike_of.append(spike_half[:, j, :])
+                nc.sync.dma_start(window[:], base_blocks[g * GROUP + j])
+                v_of.append(v_group[:, j, :])
+                spike_of.append(spike_group[:, j, :])
                 window_of.append(window)
 
-        b_of, reset_of = [], []
         for i in range(SAMPLE_BLOCKS):
             current = psum.tile([P, N], F32, name="current")
             for k in range(FEATURE_BLOCKS):
@@ -66,16 +64,11 @@ def tile_rsnn_kernel(tc, base, x, w, old_v, old_spike, offs, out):
                     start=(k == 0),
                     stop=(k == FEATURE_BLOCKS - 1),
                 )
-            b = terms.tile([P, N], F32, name="b")
+            b = work.tile([P, N], F32, name="b")
             nc.scalar.activation(b[:], current[:], COPY, bias=LEAK * BIAS, scale=LEAK)
-            reset = terms.tile([P, N], F32, name="reset")
+            reset = work.tile([P, N], F32, name="reset")
             nc.scalar.mul(reset[:], spike_of[i], RESET)
-            b_of.append(b)
-            reset_of.append(reset)
-
-        for i in range(SAMPLE_BLOCKS):
             a = work.tile([P, N], F32, name="a")
-            nc.vector.scalar_tensor_tensor(a[:], v_of[i], DECAY, reset_of[i][:], MULT, ADD)
-            nc.vector.tensor_tensor(window_of[i][:].indirect(offsets[:]), a[:], b_of[i][:], ADD)
-            store_queue = nc.sync if i % 2 == 0 else nc.scalar
-            store_queue.dma_start(out_blocks[i], window_of[i][:])
+            nc.vector.scalar_tensor_tensor(a[:], v_of[i], DECAY, reset[:], MULT, ADD)
+            nc.vector.tensor_tensor(window_of[i][:].indirect(offsets[:]), a[:], b[:], ADD)
+            nc.sync.dma_start(out_blocks[i], window_of[i][:])

@@ -4,7 +4,7 @@ P = 128
 C, S, N, F = 1024, 1024, 256, 512
 SAMPLE_BLOCKS = C // P
 FEATURE_BLOCKS = F // P
-GROUP = 2
+GROUP = 8
 
 DECAY = 0.951229424500714
 LEAK = 1.0 - DECAY

@@ -4,7 +4,7 @@ P = 128
 C, S, N, F = 1024, 1024, 256, 512
 SAMPLE_BLOCKS = C // P
 FEATURE_BLOCKS = F // P
-GROUP = 8
+GROUP = 2
 
 DECAY = 0.951229424500714
 LEAK = 1.0 - DECAY
@@ -24,37 +24,48 @@ def tile_rsnn_kernel(tc, base, x, w, old_v, old_spike, offs, out):
     out_blocks = out.rearrange("(p i) s -> i p s", i=SAMPLE_BLOCKS)
     v_rows = old_v.rearrange("(p i) n -> p i n", i=SAMPLE_BLOCKS)
     spike_rows = old_spike.rearrange("(p i) n -> p i n", i=SAMPLE_BLOCKS)
+    w_rows = w.rearrange("(p k) n -> p k n", k=FEATURE_BLOCKS)
+    x_rows = x.rearrange("(p k) c -> p k c", k=FEATURE_BLOCKS)
 
     with (
         tc.tile_pool(name="held", bufs=1) as held,
         tc.tile_pool(name="groups", bufs=SAMPLE_BLOCKS // GROUP) as groups,
         tc.tile_pool(name="windows", bufs=SAMPLE_BLOCKS) as windows,
-        tc.tile_pool(name="work", bufs=3) as work,
+        tc.tile_pool(name="work", bufs=4) as work,
         tc.psum_pool(name="psum", bufs=4) as psum,
     ):
+        warm = held.tile([P, 1], F32, name="warm")
+        nc.vector.memset(warm[:], 0.0)
+        nc.scalar.activation(warm[:], warm[:], COPY)
+
         offsets = held.tile([P, N // 16], U16, name="offsets")
         nc.sync.dma_start(offsets[:], offs)
-
         w_sb = held.tile([P, FEATURE_BLOCKS, N], BF16, name="w_sb")
-        nc.sync.dma_start(w_sb[:], w.rearrange("(p k) n -> p k n", k=FEATURE_BLOCKS))
+        nc.sync.dma_start(w_sb[:], w_rows)
         x_sb = held.tile([P, FEATURE_BLOCKS, C], BF16, name="x_sb")
-        nc.scalar.dma_start(x_sb[:], x.rearrange("(p k) c -> p k c", k=FEATURE_BLOCKS))
+        nc.sync.dma_start(x_sb[:, : FEATURE_BLOCKS // 2, :], x_rows[:, : FEATURE_BLOCKS // 2, :])
+        nc.scalar.dma_start(x_sb[:, FEATURE_BLOCKS // 2 :, :], x_rows[:, FEATURE_BLOCKS // 2 :, :])
         x_by_block = x_sb[:].rearrange("p k (c i) -> p k i c", i=SAMPLE_BLOCKS)
 
         v_of, spike_of, window_of = [], [], []
         for g in range(SAMPLE_BLOCKS // GROUP):
-            v_group = groups.tile([P, GROUP, N], F32, name="v_group")
-            nc.sync.dma_start(v_group[:], v_rows[:, g * GROUP : (g + 1) * GROUP, :])
             spike_group = groups.tile([P, GROUP, N], F32, name="spike_group")
             nc.scalar.dma_start(spike_group[:], spike_rows[:, g * GROUP : (g + 1) * GROUP, :])
+            v_group = groups.tile([P, GROUP, N], F32, name="v_group")
+            nc.sync.dma_start(v_group[:], v_rows[:, g * GROUP : (g + 1) * GROUP, :])
             for j in range(GROUP):
                 window = windows.tile([P, S], F32, name="window")
-                nc.sync.dma_start(window[:], base_blocks[g * GROUP + j])
+                window_queue = nc.scalar if g * GROUP + j == 0 else nc.sync
+                window_queue.dma_start(window[:], base_blocks[g * GROUP + j])
                 v_of.append(v_group[:, j, :])
                 spike_of.append(spike_group[:, j, :])
                 window_of.append(window)
 
-        for i in range(SAMPLE_BLOCKS):
+        def make_terms(i):
+            reset = work.tile([P, N], F32, name="reset")
+            nc.scalar.mul(reset[:], spike_of[i], RESET)
+            a = work.tile([P, N], F32, name="a")
+            nc.vector.scalar_tensor_tensor(a[:], v_of[i], DECAY, reset[:], MULT, ADD)
             current = psum.tile([P, N], F32, name="current")
             for k in range(FEATURE_BLOCKS):
                 nc.tensor.matmul(
@@ -66,9 +77,12 @@ def tile_rsnn_kernel(tc, base, x, w, old_v, old_spike, offs, out):
                 )
             b = work.tile([P, N], F32, name="b")
             nc.scalar.activation(b[:], current[:], COPY, bias=LEAK * BIAS, scale=LEAK)
-            reset = work.tile([P, N], F32, name="reset")
-            nc.scalar.mul(reset[:], spike_of[i], RESET)
-            a = work.tile([P, N], F32, name="a")
-            nc.vector.scalar_tensor_tensor(a[:], v_of[i], DECAY, reset[:], MULT, ADD)
+            return a, b
+
+        terms = make_terms(0)
+        for i in range(SAMPLE_BLOCKS):
+            a, b = terms
+            if i + 1 < SAMPLE_BLOCKS:
+                terms = make_terms(i + 1)
             nc.vector.tensor_tensor(window_of[i][:].indirect(offsets[:]), a[:], b[:], ADD)
             nc.sync.dma_start(out_blocks[i], window_of[i][:])

@@ -4,7 +4,6 @@ P = 128
 C, S, N, F = 1024, 1024, 256, 512
 SAMPLE_BLOCKS = C // P
 FEATURE_BLOCKS = F // P
-GROUP = 2
 
 DECAY = 0.951229424500714
 LEAK = 1.0 - DECAY
@@ -29,43 +28,38 @@ def tile_rsnn_kernel(tc, base, x, w, old_v, old_spike, offs, out):
 
     with (
         tc.tile_pool(name="held", bufs=1) as held,
-        tc.tile_pool(name="groups", bufs=SAMPLE_BLOCKS // GROUP) as groups,
         tc.tile_pool(name="windows", bufs=SAMPLE_BLOCKS) as windows,
-        tc.tile_pool(name="work", bufs=4) as work,
+        tc.tile_pool(name="currents", bufs=SAMPLE_BLOCKS) as currents,
         tc.psum_pool(name="psum", bufs=4) as psum,
     ):
         warm = held.tile([P, 1], F32, name="warm")
         nc.vector.memset(warm[:], 0.0)
         nc.scalar.activation(warm[:], warm[:], COPY)
 
-        offsets = held.tile([P, N // 16], U16, name="offsets")
-        nc.sync.dma_start(offsets[:], offs)
+        spike_sb = held.tile([P, SAMPLE_BLOCKS, N], F32, name="spike_sb")
+        nc.sync.dma_start(spike_sb[:], spike_rows)
+        v_sb = held.tile([P, SAMPLE_BLOCKS, N], F32, name="v_sb")
+        nc.sync.dma_start(v_sb[:], v_rows)
         w_sb = held.tile([P, FEATURE_BLOCKS, N], BF16, name="w_sb")
         nc.sync.dma_start(w_sb[:], w_rows)
         x_sb = held.tile([P, FEATURE_BLOCKS, C], BF16, name="x_sb")
-        nc.sync.dma_start(x_sb[:, : FEATURE_BLOCKS // 2, :], x_rows[:, : FEATURE_BLOCKS // 2, :])
-        nc.scalar.dma_start(x_sb[:, FEATURE_BLOCKS // 2 :, :], x_rows[:, FEATURE_BLOCKS // 2 :, :])
+        nc.sync.dma_start(x_sb[:], x_rows)
+        offsets = held.tile([P, N // 16], U16, name="offsets")
+        nc.sync.dma_start(offsets[:], offs)
+        window_of = []
+        for i in range(SAMPLE_BLOCKS):
+            window = windows.tile([P, S], F32, name="window")
+            nc.sync.dma_start(window[:], base_blocks[i])
+            window_of.append(window)
+
+        reset = held.tile([P, SAMPLE_BLOCKS, N], F32, name="reset")
+        nc.scalar.mul(reset[:], spike_sb[:], RESET)
+        a = held.tile([P, SAMPLE_BLOCKS, N], F32, name="a")
+        nc.vector.scalar_tensor_tensor(a[:], v_sb[:], DECAY, reset[:], MULT, ADD)
+
         x_by_block = x_sb[:].rearrange("p k (c i) -> p k i c", i=SAMPLE_BLOCKS)
-
-        v_of, spike_of, window_of = [], [], []
-        for g in range(SAMPLE_BLOCKS // GROUP):
-            spike_group = groups.tile([P, GROUP, N], F32, name="spike_group")
-            nc.scalar.dma_start(spike_group[:], spike_rows[:, g * GROUP : (g + 1) * GROUP, :])
-            v_group = groups.tile([P, GROUP, N], F32, name="v_group")
-            nc.sync.dma_start(v_group[:], v_rows[:, g * GROUP : (g + 1) * GROUP, :])
-            for j in range(GROUP):
-                window = windows.tile([P, S], F32, name="window")
-                window_queue = nc.scalar if g * GROUP + j == 0 else nc.sync
-                window_queue.dma_start(window[:], base_blocks[g * GROUP + j])
-                v_of.append(v_group[:, j, :])
-                spike_of.append(spike_group[:, j, :])
-                window_of.append(window)
-
-        def make_terms(i):
-            reset = work.tile([P, N], F32, name="reset")
-            nc.scalar.mul(reset[:], spike_of[i], RESET)
-            a = work.tile([P, N], F32, name="a")
-            nc.vector.scalar_tensor_tensor(a[:], v_of[i], DECAY, reset[:], MULT, ADD)
+        b_of = []
+        for i in range(SAMPLE_BLOCKS):
             current = psum.tile([P, N], F32, name="current")
             for k in range(FEATURE_BLOCKS):
                 nc.tensor.matmul(
@@ -75,14 +69,10 @@ def tile_rsnn_kernel(tc, base, x, w, old_v, old_spike, offs, out):
                     start=(k == 0),
                     stop=(k == FEATURE_BLOCKS - 1),
                 )
-            b = work.tile([P, N], F32, name="b")
+            b = currents.tile([P, N], F32, name="b")
             nc.scalar.activation(b[:], current[:], COPY, bias=LEAK * BIAS, scale=LEAK)
-            return a, b
+            b_of.append(b)
 
-        terms = make_terms(0)
         for i in range(SAMPLE_BLOCKS):
-            a, b = terms
-            if i + 1 < SAMPLE_BLOCKS:
-                terms = make_terms(i + 1)
-            nc.vector.tensor_tensor(window_of[i][:].indirect(offsets[:]), a[:], b[:], ADD)
+            nc.vector.tensor_tensor(window_of[i][:].indirect(offsets[:]), a[:, i, :], b_of[i][:], ADD)
             nc.sync.dma_start(out_blocks[i], window_of[i][:])

@@ -4,6 +4,7 @@ P = 128
 C, S, N, F = 1024, 1024, 256, 512
 SAMPLE_BLOCKS = C // P
 FEATURE_BLOCKS = F // P
+HALF = SAMPLE_BLOCKS // 2
 
 DECAY = 0.951229424500714
 LEAK = 1.0 - DECAY
@@ -28,6 +29,7 @@ def tile_rsnn_kernel(tc, base, x, w, old_v, old_spike, offs, out):
 
     with (
         tc.tile_pool(name="held", bufs=1) as held,
+        tc.tile_pool(name="halves", bufs=2) as halves,
         tc.tile_pool(name="windows", bufs=SAMPLE_BLOCKS) as windows,
         tc.tile_pool(name="currents", bufs=SAMPLE_BLOCKS) as currents,
         tc.psum_pool(name="psum", bufs=4) as psum,
@@ -36,26 +38,35 @@ def tile_rsnn_kernel(tc, base, x, w, old_v, old_spike, offs, out):
         nc.vector.memset(warm[:], 0.0)
         nc.scalar.activation(warm[:], warm[:], COPY)
 
-        spike_sb = held.tile([P, SAMPLE_BLOCKS, N], F32, name="spike_sb")
-        nc.sync.dma_start(spike_sb[:], spike_rows)
-        v_sb = held.tile([P, SAMPLE_BLOCKS, N], F32, name="v_sb")
-        nc.sync.dma_start(v_sb[:], v_rows)
         w_sb = held.tile([P, FEATURE_BLOCKS, N], BF16, name="w_sb")
-        nc.sync.dma_start(w_sb[:], w_rows)
         x_sb = held.tile([P, FEATURE_BLOCKS, C], BF16, name="x_sb")
-        nc.sync.dma_start(x_sb[:], x_rows)
         offsets = held.tile([P, N // 16], U16, name="offsets")
-        nc.sync.dma_start(offsets[:], offs)
-        window_of = []
-        for i in range(SAMPLE_BLOCKS):
-            window = windows.tile([P, S], F32, name="window")
-            nc.sync.dma_start(window[:], base_blocks[i])
-            window_of.append(window)
+        spike_of, v_of, window_of = [], [], []
+        for h in range(2):
+            blocks = slice(h * HALF, (h + 1) * HALF)
+            spike_half = halves.tile([P, HALF, N], F32, name="spike_half")
+            nc.sync.dma_start(spike_half[:], spike_rows[:, blocks, :])
+            v_half = halves.tile([P, HALF, N], F32, name="v_half")
+            nc.sync.dma_start(v_half[:], v_rows[:, blocks, :])
+            spike_of.append(spike_half)
+            v_of.append(v_half)
+            if h == 0:
+                nc.sync.dma_start(w_sb[:], w_rows)
+                nc.sync.dma_start(x_sb[:], x_rows)
+                nc.sync.dma_start(offsets[:], offs)
+            for i in range(h * HALF, (h + 1) * HALF):
+                window = windows.tile([P, S], F32, name="window")
+                nc.sync.dma_start(window[:], base_blocks[i])
+                window_of.append(window)
 
-        reset = held.tile([P, SAMPLE_BLOCKS, N], F32, name="reset")
-        nc.scalar.mul(reset[:], spike_sb[:], RESET)
-        a = held.tile([P, SAMPLE_BLOCKS, N], F32, name="a")
-        nc.vector.scalar_tensor_tensor(a[:], v_sb[:], DECAY, reset[:], MULT, ADD)
+        def make_a(h):
+            reset = halves.tile([P, HALF, N], F32, name="reset")
+            nc.scalar.mul(reset[:], spike_of[h][:], RESET)
+            a = halves.tile([P, HALF, N], F32, name="a")
+            nc.vector.scalar_tensor_tensor(a[:], v_of[h][:], DECAY, reset[:], MULT, ADD)
+            return a
+
+        a_of = [make_a(0)]
 
         x_by_block = x_sb[:].rearrange("p k (c i) -> p k i c", i=SAMPLE_BLOCKS)
         b_of = []
@@ -74,5 +85,9 @@ def tile_rsnn_kernel(tc, base, x, w, old_v, old_spike, offs, out):
             b_of.append(b)
 
         for i in range(SAMPLE_BLOCKS):
-            nc.vector.tensor_tensor(window_of[i][:].indirect(offsets[:]), a[:, i, :], b_of[i][:], ADD)
+            if i == HALF:
+                a_of.append(make_a(1))
+            nc.vector.tensor_tensor(
+                window_of[i][:].indirect(offsets[:]), a_of[i // HALF][:, i % HALF, :], b_of[i][:], ADD
+            )
             nc.sync.dma_start(out_blocks[i], window_of[i][:])

@@ -5,6 +5,7 @@ C, S, N, F = 1024, 1024, 256, 512
 SAMPLE_BLOCKS = C // P
 FEATURE_BLOCKS = F // P
 HALF = SAMPLE_BLOCKS // 2
+DMA_ALIGN = 256
 
 DECAY = 0.951229424500714
 LEAK = 1.0 - DECAY
@@ -38,15 +39,15 @@ def tile_rsnn_kernel(tc, base, x, w, old_v, old_spike, offs, out):
         nc.vector.memset(warm[:], 0.0)
         nc.scalar.activation(warm[:], warm[:], COPY)
 
-        w_sb = held.tile([P, FEATURE_BLOCKS, N], BF16, name="w_sb")
-        x_sb = held.tile([P, FEATURE_BLOCKS, C], BF16, name="x_sb")
+        w_sb = held.tile([P, FEATURE_BLOCKS, N], BF16, name="w_sb", align_bytes=DMA_ALIGN)
+        x_sb = held.tile([P, FEATURE_BLOCKS, C], BF16, name="x_sb", align_bytes=DMA_ALIGN)
         offsets = held.tile([P, N // 16], U16, name="offsets")
         spike_of, v_of, window_of = [], [], []
         for h in range(2):
             blocks = slice(h * HALF, (h + 1) * HALF)
-            spike_half = halves.tile([P, HALF, N], F32, name="spike_half")
+            spike_half = halves.tile([P, HALF, N], F32, name="spike_half", align_bytes=DMA_ALIGN)
             nc.sync.dma_start(spike_half[:], spike_rows[:, blocks, :])
-            v_half = halves.tile([P, HALF, N], F32, name="v_half")
+            v_half = halves.tile([P, HALF, N], F32, name="v_half", align_bytes=DMA_ALIGN)
             nc.sync.dma_start(v_half[:], v_rows[:, blocks, :])
             spike_of.append(spike_half)
             v_of.append(v_half)
@@ -55,7 +56,7 @@ def tile_rsnn_kernel(tc, base, x, w, old_v, old_spike, offs, out):
                 nc.sync.dma_start(x_sb[:], x_rows)
                 nc.sync.dma_start(offsets[:], offs)
             for i in range(h * HALF, (h + 1) * HALF):
-                window = windows.tile([P, S], F32, name="window")
+                window = windows.tile([P, S], F32, name="window", align_bytes=DMA_ALIGN)
                 nc.sync.dma_start(window[:], base_blocks[i])
                 window_of.append(window)
 

@@ -21,10 +21,10 @@ COPY = mybir.ActivationFunctionType.Copy
 
 def tile_rsnn_kernel(tc, base, x, w, old_v, old_spike, offs, out):
     nc = tc.nc
-    base_blocks = base.rearrange("(p i) s -> i p s", i=SAMPLE_BLOCKS)
-    out_blocks = out.rearrange("(p i) s -> i p s", i=SAMPLE_BLOCKS)
-    v_rows = old_v.rearrange("(p i) n -> p i n", i=SAMPLE_BLOCKS)
-    spike_rows = old_spike.rearrange("(p i) n -> p i n", i=SAMPLE_BLOCKS)
+    base_blocks = base.rearrange("(h p i) s -> h i p s", p=P, i=HALF)
+    out_blocks = out.rearrange("(h p i) s -> h i p s", p=P, i=HALF)
+    v_rows = old_v.rearrange("(h p i) n -> h p i n", p=P, i=HALF)
+    spike_rows = old_spike.rearrange("(h p i) n -> h p i n", p=P, i=HALF)
     w_rows = w.rearrange("(p k) n -> p k n", k=FEATURE_BLOCKS)
     x_rows = x.rearrange("(p k) c -> p k c", k=FEATURE_BLOCKS)
 
@@ -44,20 +44,19 @@ def tile_rsnn_kernel(tc, base, x, w, old_v, old_spike, offs, out):
         offsets = held.tile([P, N // 16], U16, name="offsets")
         spike_of, v_of, window_of = [], [], []
         for h in range(2):
-            blocks = slice(h * HALF, (h + 1) * HALF)
             spike_half = halves.tile([P, HALF, N], F32, name="spike_half", align_bytes=DMA_ALIGN)
-            nc.sync.dma_start(spike_half[:], spike_rows[:, blocks, :])
+            nc.sync.dma_start(spike_half[:], spike_rows[h])
             v_half = halves.tile([P, HALF, N], F32, name="v_half", align_bytes=DMA_ALIGN)
-            nc.sync.dma_start(v_half[:], v_rows[:, blocks, :])
+            nc.sync.dma_start(v_half[:], v_rows[h])
             spike_of.append(spike_half)
             v_of.append(v_half)
             if h == 0:
                 nc.sync.dma_start(w_sb[:], w_rows)
                 nc.sync.dma_start(x_sb[:], x_rows)
                 nc.sync.dma_start(offsets[:], offs)
-            for i in range(h * HALF, (h + 1) * HALF):
+            for i in range(HALF):
                 window = windows.tile([P, S], F32, name="window", align_bytes=DMA_ALIGN)
-                nc.sync.dma_start(window[:], base_blocks[i])
+                nc.sync.dma_start(window[:], base_blocks[h, i])
                 window_of.append(window)
 
         def make_a(h):
@@ -69,14 +68,14 @@ def tile_rsnn_kernel(tc, base, x, w, old_v, old_spike, offs, out):
 
         a_of = [make_a(0)]
 
-        x_by_block = x_sb[:].rearrange("p k (c i) -> p k i c", i=SAMPLE_BLOCKS)
+        x_by_block = x_sb[:].rearrange("p k (h c i) -> p k h i c", c=P, i=HALF)
         b_of = []
         for i in range(SAMPLE_BLOCKS):
             current = psum.tile([P, N], F32, name="current")
             for k in range(FEATURE_BLOCKS):
                 nc.tensor.matmul(
                     current[:],
-                    x_by_block[:, k, i, :],
+                    x_by_block[:, k, i // HALF, i % HALF, :],
                     w_sb[:, k, :],
                     start=(k == 0),
                     stop=(k == FEATURE_BLOCKS - 1),
@@ -91,4 +90,4 @@ def tile_rsnn_kernel(tc, base, x, w, old_v, old_spike, offs, out):
             nc.vector.tensor_tensor(
                 window_of[i][:].indirect(offsets[:]), a_of[i // HALF][:, i % HALF, :], b_of[i][:], ADD
             )
-            nc.sync.dma_start(out_blocks[i], window_of[i][:])
+            nc.sync.dma_start(out_blocks[i // HALF, i % HALF], window_of[i][:])

import concourse.mybir as mybir

P = 128
C, S, N, F = 1024, 1024, 256, 512
SAMPLE_BLOCKS = C // P
FEATURE_BLOCKS = F // P
HALF = SAMPLE_BLOCKS // 2
DMA_ALIGN = 256

DECAY = 0.951229424500714
LEAK = 1.0 - DECAY
RESET = -0.03
BIAS = 0.49996052210190806

FLOPS = 2 * C * N * F

BF16, F32, U16 = mybir.dt.bfloat16, mybir.dt.float32, mybir.dt.uint16
MULT, ADD = mybir.AluOpType.mult, mybir.AluOpType.add
COPY = mybir.ActivationFunctionType.Copy


def tile_rsnn_kernel(tc, base, x, w, old_v, old_spike, offs, out):
    nc = tc.nc
    base_blocks = base.rearrange("(h p i) s -> h i p s", p=P, i=HALF)
    out_blocks = out.rearrange("(h p i) s -> h i p s", p=P, i=HALF)
    v_rows = old_v.rearrange("(h p i) n -> h p i n", p=P, i=HALF)
    spike_rows = old_spike.rearrange("(h p i) n -> h p i n", p=P, i=HALF)
    w_rows = w.rearrange("(p k) n -> p k n", k=FEATURE_BLOCKS)
    x_rows = x.rearrange("(p k) c -> p k c", k=FEATURE_BLOCKS)

    with (
        tc.tile_pool(name="held", bufs=1) as held,
        tc.tile_pool(name="halves", bufs=2) as halves,
        tc.tile_pool(name="windows", bufs=SAMPLE_BLOCKS) as windows,
        tc.tile_pool(name="currents", bufs=SAMPLE_BLOCKS) as currents,
        tc.psum_pool(name="psum", bufs=4) as psum,
    ):
        warm = held.tile([P, 1], F32, name="warm")
        nc.vector.memset(warm[:], 0.0)
        nc.scalar.activation(warm[:], warm[:], COPY)

        w_sb = held.tile([P, FEATURE_BLOCKS, N], BF16, name="w_sb", align_bytes=DMA_ALIGN)
        x_sb = held.tile([P, FEATURE_BLOCKS, C], BF16, name="x_sb", align_bytes=DMA_ALIGN)
        offsets = held.tile([P, N // 16], U16, name="offsets")
        spike_of, v_of, window_of = [], [], []
        for h in range(2):
            spike_half = halves.tile([P, HALF, N], F32, name="spike_half", align_bytes=DMA_ALIGN)
            nc.sync.dma_start(spike_half[:], spike_rows[h])
            v_half = halves.tile([P, HALF, N], F32, name="v_half", align_bytes=DMA_ALIGN)
            nc.sync.dma_start(v_half[:], v_rows[h])
            spike_of.append(spike_half)
            v_of.append(v_half)
            if h == 0:
                nc.sync.dma_start(w_sb[:], w_rows)
                nc.sync.dma_start(x_sb[:], x_rows)
                nc.sync.dma_start(offsets[:], offs)
            for i in range(HALF):
                window = windows.tile([P, S], F32, name="window", align_bytes=DMA_ALIGN)
                nc.sync.dma_start(window[:], base_blocks[h, i])
                window_of.append(window)

        def make_a(h):
            reset = halves.tile([P, HALF, N], F32, name="reset")
            nc.scalar.mul(reset[:], spike_of[h][:], RESET)
            a = halves.tile([P, HALF, N], F32, name="a")
            nc.vector.scalar_tensor_tensor(a[:], v_of[h][:], DECAY, reset[:], MULT, ADD)
            return a

        a_of = [make_a(0)]

        x_by_block = x_sb[:].rearrange("p k (h c i) -> p k h i c", c=P, i=HALF)
        b_of = []
        for i in range(SAMPLE_BLOCKS):
            current = psum.tile([P, N], F32, name="current")
            for k in range(FEATURE_BLOCKS):
                nc.tensor.matmul(
                    current[:],
                    x_by_block[:, k, i // HALF, i % HALF, :],
                    w_sb[:, k, :],
                    start=(k == 0),
                    stop=(k == FEATURE_BLOCKS - 1),
                )
            b = currents.tile([P, N], F32, name="b")
            nc.scalar.activation(b[:], current[:], COPY, bias=LEAK * BIAS, scale=LEAK)
            b_of.append(b)

        for i in range(SAMPLE_BLOCKS):
            if i == HALF:
                a_of.append(make_a(1))
            nc.vector.tensor_tensor(
                window_of[i][:].indirect(offsets[:]), a_of[i // HALF][:, i % HALF, :], b_of[i][:], ADD
            )
            nc.sync.dma_start(out_blocks[i // HALF, i % HALF], window_of[i][:])
